import numpy as np
import ml_dtypes


def mxq(x, axis, fmt="e4m3"):
    dtype, down = {"e4m3": (ml_dtypes.float8_e4m3fn, 7), "e5m2": (ml_dtypes.float8_e5m2, 14)}[fmt]
    v = np.moveaxis(np.asarray(x, np.float32).astype(ml_dtypes.bfloat16).astype(np.float64), axis, -1)
    blocks = v.reshape(v.shape[:-1] + (-1, 32))
    amax = np.abs(blocks).max(-1, keepdims=True)
    byte = np.maximum(np.where(amax > 0, np.frexp(amax)[1] - 1 + 127, 0) - down, 1)
    scale = np.exp2(byte - 127.0)
    codes = (blocks / scale).astype(np.float32).astype(dtype).astype(np.float64)
    return np.moveaxis((codes * scale).reshape(v.shape), -1, axis)


WIDE = False


def mx_kscale(k):
    if not WIDE:
        return np.ones(k)
    levels = np.array([10, -10, 5, -5, 0])
    if k % 512:
        return np.exp2(np.random.permutation(np.resize(levels, k // 32))).repeat(32)
    a = np.empty((k // 512, 16))
    for p in range(k // 512):
        a[p, :8] = np.random.permutation(np.resize(levels, 8))
        for g in range(8):
            far = levels[np.abs(levels - a[p, g]) >= 10]
            a[p, g + 8] = far[np.random.randint(len(far))]
    return np.exp2(a.ravel()).repeat(32)


BF16 = ml_dtypes.bfloat16


def bf(x):
    return np.asarray(x, np.float32).astype(BF16)


def f64(x):
    return np.asarray(x).astype(np.float64)


B, S, D, H, HD, FF = 2, 256, 1024, 8, 128, 4096
ROT = HD // 4
EPS = 1e-5
ROPE_BASE = 10000.0


def layernorm(x, g, b):
    mu = x.mean(-1, keepdims=True)
    var = np.square(x - mu).mean(-1, keepdims=True)
    return (x - mu) / np.sqrt(var + EPS) * g + b


def rope_cos_sin():
    inv_freq = 1.0 / ROPE_BASE ** (np.arange(0, ROT, 2) / ROT)
    freqs = np.outer(np.arange(S), inv_freq)
    emb = np.concatenate([freqs, freqs], -1)
    return np.cos(emb), np.sin(emb)


def apply_rope(x, cos, sin):
    half = x.shape[-1] // 2
    x1, x2 = x[..., :half], x[..., half:]
    rot = np.concatenate([-x2, x1], -1)
    return x * cos[None, None, :, :] + rot * sin[None, None, :, :]


def setup_inputs():
    s = mx_kscale(D)
    return {"hidden_states": bf(np.random.standard_normal((B, S, D))),
            "ln1_g": bf((1.0 + 0.1 * np.random.standard_normal(D)) * s),
            "ln1_b": bf(0.1 * np.random.standard_normal(D) * s),
            "W_qkv": bf(np.random.standard_normal((D, 3 * H * HD)) / np.sqrt(D) / s[:, None]),
            "b_qkv": bf(0.3 * np.random.standard_normal(3 * H * HD))}


def reference(hidden_states, ln1_g, ln1_b, W_qkv, b_qkv):
    x = layernorm(f64(hidden_states), f64(ln1_g), f64(ln1_b))
    qkv = ((mxq(x, 2, "e4m3") @ mxq(f64(W_qkv), 0, "e4m3")) + f64(b_qkv)).reshape(B, S, H, 3 * HD)
    q = np.transpose(qkv[..., :HD], (0, 2, 1, 3))
    k = np.transpose(qkv[..., HD:2 * HD], (0, 2, 1, 3))
    v = np.transpose(qkv[..., 2 * HD:], (0, 2, 1, 3))
    cos, sin = rope_cos_sin()
    q = np.concatenate([apply_rope(q[..., :ROT], cos, sin), q[..., ROT:]], -1)
    k = np.concatenate([apply_rope(k[..., :ROT], cos, sin), k[..., ROT:]], -1)
    return q, k, v

@@ -1,0 +1,352 @@
+import math
+from contextlib import ExitStack
+
+import concourse.mybir as mybir
+from concourse.masks import make_identity
+
+F32 = mybir.dt.float32
+BF16 = mybir.dt.bfloat16
+I32 = mybir.dt.int32
+U32 = mybir.dt.uint32
+U8 = mybir.dt.uint8
+FP8X4 = mybir.dt.float8_e4m3fn_x4
+ALU = mybir.AluOpType
+ACT = mybir.ActivationFunctionType
+
+P = 128
+B, S, D, H, HD = 2, 256, 1024, 8, 128
+ROT = HD // 4
+HALF = ROT // 2
+EPS = 1e-5
+ROPE_BASE = 10000.0
+PACK = 4
+PASSES = D // (P * PACK)
+K_CHUNKS = D // P
+PARITY = S // P
+CHUNK_HEADS = 2
+CHUNKS = H // CHUNK_HEADS
+CHUNK_BLOCKS = 3 * CHUNK_HEADS
+CHUNK_COLS = CHUNK_BLOCKS * HD
+WIDE_BLOCKS = 4
+WIDE_COLS = WIDE_BLOCKS * HD
+BN_FMAX = 512
+BN_STATS_DIM = 6
+ROUND_MAGIC = 1.5 * 2.0**23
+
+FLOPS = 2 * B * S * D * 3 * H * HD
+
+
+def regroup(copy, dst, src):
+    copy(
+        out=dst.rearrange("p (c i) t -> p c t i", i=4),
+        in_=src.rearrange("p t (c i) -> p c t i", i=4),
+    )
+
+
+def tile_customgptneoxlayer_pa_kernel(
+    tc, hidden_states, ln1_g, ln1_b, W_qkv, b_qkv, out_0, out_1, out_2
+):
+    nc = tc.nc
+    outs = (out_0, out_1, out_2)
+    wide = slice(0, WIDE_COLS)
+    narrow = slice(WIDE_COLS, CHUNK_COLS)
+    with ExitStack() as stack:
+        consts = stack.enter_context(tc.tile_pool(name="consts", bufs=1))
+        xpool = stack.enter_context(tc.tile_pool(name="xpool", bufs=1))
+        wpool = stack.enter_context(tc.tile_pool(name="wpool", bufs=1))
+        stage = stack.enter_context(tc.tile_pool(name="stage", bufs=3))
+        respool = stack.enter_context(tc.tile_pool(name="respool", bufs=1))
+        ropepool = stack.enter_context(tc.tile_pool(name="ropepool", bufs=2))
+        psum = stack.enter_context(tc.psum_pool(name="psum", bufs=8))
+        stack.enter_context(tc.manual_schedule())
+
+        gain_raw = consts.tile([P, PASSES, PACK], BF16)
+        shift_raw = consts.tile([P, PASSES, PACK], BF16)
+        x_sb = [xpool.tile([P, PARITY, D], BF16, name="x_sb%d" % b) for b in range(B)]
+        xn = [xpool.tile([P, PARITY, D], F32, name="xn%d" % b) for b in range(B)]
+        wraw = [
+            [wpool.tile([P, PACK, CHUNK_COLS], BF16, name="wraw%d_%d" % (c, g)) for g in range(PASSES)]
+            for c in range(CHUNKS)
+        ]
+        bias_bc = [consts.tile([P, CHUNK_BLOCKS, HD], BF16, name="bias_bc%d" % c) for c in range(CHUNKS)]
+        wcodes = [
+            wpool.tile([P, PASSES, CHUNK_COLS], U32, name="wcodes%d" % c, align_bytes=64)
+            for c in range(CHUNKS)
+        ]
+        wscales = [
+            wpool.tile([P, PASSES, CHUNK_COLS], U8, name="wscales%d" % c, align_bytes=64)
+            for c in range(CHUNKS)
+        ]
+        xb = xpool.tile([P, B, K_CHUNKS, S], BF16)
+        xcodes = xpool.tile([P, B, PASSES, S], U32, align_bytes=64)
+        xscales = xpool.tile([P, B, PASSES, S], U8, align_bytes=64)
+        res = [
+            respool.tile([P, B, CHUNK_HEADS, 3, PARITY, HD], F32, name="res%d" % c)
+            for c in range(CHUNKS)
+        ]
+
+        def load_x(b):
+            rows = hidden_states[b].rearrange("(p e) d -> p e d", e=PARITY)
+            for e in range(PARITY):
+                nc.sync.dma_start(out=x_sb[b][:, e, :], in_=rows[:, e, :])
+
+        w_rows = W_qkv.rearrange("(g p t) n -> g p t n", t=PACK, p=P)
+
+        def load_w(c, g):
+            nc.sync.dma_start(
+                out=wraw[c][g][:], in_=w_rows[g][:, :, CHUNK_COLS * c : CHUNK_COLS * (c + 1)]
+            )
+
+        load_x(0)
+        for raw, param in ((gain_raw, ln1_g), (shift_raw, ln1_b)):
+            nc.sync.dma_start(
+                out=raw[:], in_=param.rearrange("(g p t) -> p g t", t=PACK, p=P)
+            )
+        load_w(0, 0)
+        load_x(1)
+        load_w(0, 1)
+        for c in range(CHUNKS):
+            nc.sync.dma_start(
+                out=bias_bc[c][:].rearrange("p n d -> p (n d)"),
+                in_=b_qkv[CHUNK_COLS * c : CHUNK_COLS * (c + 1)].partition_broadcast(P),
+            )
+            if c + 1 < CHUNKS:
+                for g in range(PASSES):
+                    load_w(c + 1, g)
+
+        pos_i = consts.tile([P, PARITY], I32)
+        nc.gpsimd.iota(pos_i[:], pattern=[[1, PARITY]], base=0, channel_multiplier=PARITY)
+        ident_f32 = consts.tile([P, P], F32)
+        make_identity(nc, ident_f32[:])
+        neg_half = consts.tile([P, PARITY], F32)
+        nc.vector.memset(neg_half[:], -0.5)
+
+        pos = consts.tile([P, PARITY], F32)
+        nc.vector.tensor_copy(out=pos[:], in_=pos_i[:])
+        turns = consts.tile([P, 2, PARITY, HALF], F32)
+        for j in range(HALF):
+            nc.vector.tensor_scalar(
+                out=turns[:, 1, :, j],
+                in0=pos[:],
+                scalar1=ROPE_BASE ** (-j / HALF) / (2.0 * math.pi),
+                scalar2=None,
+                op0=ALU.mult,
+            )
+        nc.vector.tensor_scalar(
+            out=turns[:, 0], in0=turns[:, 1], scalar1=0.25, scalar2=None, op0=ALU.add
+        )
+        whole = consts.tile([P, 2, PARITY, HALF], F32)
+        nc.vector.tensor_scalar(
+            out=whole[:],
+            in0=turns[:],
+            scalar1=ROUND_MAGIC,
+            scalar2=ROUND_MAGIC,
+            op0=ALU.add,
+            op1=ALU.subtract,
+        )
+        frac = consts.tile([P, 2, PARITY, HALF], F32)
+        nc.vector.tensor_tensor(out=frac[:], in0=turns[:], in1=whole[:], op=ALU.subtract)
+        cos_tab = consts.tile([P, PARITY, 2, HALF], F32)
+        sin_tab = consts.tile([P, PARITY, 2, HALF], F32)
+        nc.scalar.activation(
+            out=cos_tab[:],
+            in_=frac[:, 0].unsqueeze(2).to_broadcast([P, PARITY, 2, HALF]),
+            func=ACT.Sin,
+            scale=2.0 * math.pi,
+        )
+        nc.scalar.activation(
+            out=sin_tab[:, :, 0, :], in_=frac[:, 1], func=ACT.Sin, scale=-2.0 * math.pi
+        )
+        nc.scalar.activation(
+            out=sin_tab[:, :, 1, :], in_=frac[:, 1], func=ACT.Sin, scale=2.0 * math.pi
+        )
+        cos_qk = consts.tile([P, 2, PARITY, ROT], F32)
+        sin_qk = consts.tile([P, 2, PARITY, ROT], F32)
+        gb_cols = consts.tile([P, 2 * K_CHUNKS], F32)
+
+        def statistics(b):
+            stats = xpool.tile([P, PARITY, D // BN_FMAX, BN_STATS_DIM], F32, name="stats%d" % b)
+            mean_var = xpool.tile([P, PARITY, 2], F32, name="mean_var%d" % b)
+            for e in range(PARITY):
+                for f in range(D // BN_FMAX):
+                    nc.vector.bn_stats(
+                        out=stats[:, e, f, :], in_=x_sb[b][:, e, BN_FMAX * f : BN_FMAX * (f + 1)]
+                    )
+                nc.vector.bn_aggr(
+                    out=mean_var[:, e, :], in_=stats[:, e].rearrange("p f s -> p (f s)")
+                )
+            neg_mean = xpool.tile([P, PARITY], F32, name="neg_mean%d" % b)
+            nc.vector.tensor_scalar(
+                out=neg_mean[:], in0=mean_var[:, :, 0], scalar1=-1.0, scalar2=None, op0=ALU.mult
+            )
+            var_eps = xpool.tile([P, PARITY], F32, name="var_eps%d" % b)
+            nc.vector.tensor_scalar(
+                out=var_eps[:], in0=mean_var[:, :, 1], scalar1=EPS, scalar2=None, op0=ALU.add
+            )
+            rstd = xpool.tile([P, PARITY], F32, name="rstd%d" % b)
+            nc.gpsimd.tensor_tensor(out=rstd[:], in0=var_eps[:], in1=neg_half[:], op=ALU.pow)
+            for e in range(PARITY):
+                nc.gpsimd.tensor_scalar(
+                    out=xn[b][:, e, :].rearrange("p (g t q) -> p g t q", g=PASSES, t=PACK),
+                    in0=x_sb[b][:, e, :].rearrange("p (g q t) -> p g t q", g=PASSES, t=PACK),
+                    scalar1=neg_mean[:, e : e + 1],
+                    scalar2=rstd[:, e : e + 1],
+                    op0=ALU.add,
+                    op1=ALU.mult,
+                )
+
+        def transpose_x(b):
+            for i in range(K_CHUNKS // 2):
+                xt = psum.tile([P, 2, S], F32, tag="bank", name="xt%d_%d" % (b, i))
+                for ai in range(2):
+                    a = 2 * i + ai
+                    for e in range(PARITY):
+                        nc.tensor.transpose(
+                            xt[:, ai, P * e : P * (e + 1)],
+                            xn[b][:, e, P * a : P * (a + 1)],
+                            ident_f32[:],
+                        )
+                for ai in range(2):
+                    a = 2 * i + ai
+                    nc.vector.tensor_scalar(
+                        out=xb[:, b, a, :],
+                        in0=xt[:, ai, :],
+                        scalar1=gb_cols[:, a : a + 1],
+                        scalar2=gb_cols[:, K_CHUNKS + a : K_CHUNKS + a + 1],
+                        op0=ALU.mult,
+                        op1=ALU.add,
+                    )
+
+        def quantise_x(b):
+            xg = xpool.tile([P, PASSES, S, PACK], BF16, name="xg%d" % b, align_bytes=64)
+            for g in range(PASSES):
+                regroup(nc.vector.tensor_copy, xg[:, g], xb[:, b, PACK * g : PACK * (g + 1), :])
+            nc.vector.quantize_mx(
+                out=xcodes[:, b].rearrange("p g c -> p (g c)").bitcast(FP8X4),
+                scales=xscales[:, b].rearrange("p g c -> p (g c)"),
+                in_=xg[:].rearrange("p g c t -> p (g c t)"),
+            )
+
+        def prepare_w(c, g):
+            wg = stage.tile([P, CHUNK_COLS, PACK], BF16, align_bytes=64, name="wg")
+            for part in (wide, narrow):
+                regroup(nc.scalar.copy, wg[:, part, :], wraw[c][g][:, :, part])
+            for part in (wide, narrow):
+                nc.vector.quantize_mx(
+                    out=wcodes[c][:, g, part].bitcast(FP8X4),
+                    scales=wscales[c][:, g, part],
+                    in_=wg[:, part, :].rearrange("p c t -> p (c t)"),
+                )
+
+        def mx_group(acc, b, e, c, part):
+            tokens = slice(P * e, P * (e + 1))
+            for g in range(PASSES):
+                nc.tensor.matmul_mx(
+                    out=acc,
+                    lhsT=xcodes[:, b, g, tokens].bitcast(FP8X4),
+                    lhsT_scale=xscales[:, b, g, tokens],
+                    rhs=wcodes[c][:, g, part].bitcast(FP8X4),
+                    rhs_scale=wscales[c][:, g, part],
+                    start=(g == 0),
+                    stop=(g == PASSES - 1),
+                )
+
+        def store(c, b, w):
+            heads = slice(CHUNK_HEADS * c, CHUNK_HEADS * (c + 1))
+            nc.sync.dma_start(
+                out=outs[w][b, heads].rearrange("h (p e) d -> p h (e d)", e=PARITY),
+                in_=res[c][:, b, :, w].rearrange("p h e d -> p h (e d)"),
+            )
+
+        def project(c, b):
+            blocks = res[c][:, b].rearrange("p h w e d -> p (h w) e d")
+            n_narrow = CHUNK_BLOCKS - WIDE_BLOCKS
+            acc_wide = []
+            for e in range(PARITY):
+                acc = psum.tile([P, WIDE_BLOCKS, HD], F32, tag="bank", name="acc_wide%d" % e)
+                mx_group(acc[:].rearrange("p n d -> p (n d)"), b, e, c, wide)
+                acc_wide.append(acc)
+            acc_narrow = psum.tile([P, PARITY, n_narrow, HD], F32, tag="bank")
+            for e in range(PARITY):
+                mx_group(acc_narrow[:, e].rearrange("p n d -> p (n d)"), b, e, c, narrow)
+            for e in range(PARITY):
+                nc.vector.tensor_tensor(
+                    out=blocks[:, 0:WIDE_BLOCKS, e, :],
+                    in0=acc_wide[e][:],
+                    in1=bias_bc[c][:, 0:WIDE_BLOCKS, :],
+                    op=ALU.add,
+                )
+            nc.vector.tensor_tensor(
+                out=blocks[:, WIDE_BLOCKS:CHUNK_BLOCKS].rearrange("p n e d -> p e n d"),
+                in0=acc_narrow[:],
+                in1=bias_bc[c][:, WIDE_BLOCKS:CHUNK_BLOCKS, :]
+                .unsqueeze(1)
+                .to_broadcast([P, PARITY, n_narrow, HD]),
+                op=ALU.add,
+            )
+            store(c, b, 2)
+
+        def rotate(engine, c, first_b, n_b):
+            u = res[c][:, first_b : first_b + n_b, :, 0:2, :, 0:ROT].rearrange(
+                "p b h w e j -> p (b h) (w e) j"
+            )
+            shape = [P, n_b * CHUNK_HEADS, 2 * PARITY, ROT]
+            cos_b = cos_qk[:].rearrange("p w e j -> p (w e) j").unsqueeze(1).to_broadcast(shape)
+            sin_b = sin_qk[:].rearrange("p w e j -> p (w e) j").unsqueeze(1).to_broadcast(shape)
+            straight = ropepool.tile(shape, F32, tag="straight")
+            crossed = ropepool.tile(shape, F32, tag="crossed")
+            engine.tensor_tensor(out=straight[:], in0=u, in1=cos_b, op=ALU.mult)
+            engine.tensor_tensor(
+                out=crossed[:, :, :, 0:HALF],
+                in0=u[:, :, :, HALF:ROT],
+                in1=sin_b[:, :, :, 0:HALF],
+                op=ALU.mult,
+            )
+            engine.tensor_tensor(
+                out=crossed[:, :, :, HALF:ROT],
+                in0=u[:, :, :, 0:HALF],
+                in1=sin_b[:, :, :, HALF:ROT],
+                op=ALU.mult,
+            )
+            engine.tensor_tensor(out=u, in0=straight[:], in1=crossed[:], op=ALU.add)
+
+        def store_qk(c, b):
+            store(c, b, 0)
+            store(c, b, 1)
+
+        statistics(0)
+        for i, raw in enumerate((gain_raw, shift_raw)):
+            nc.vector.tensor_copy(
+                out=gb_cols[:, K_CHUNKS * i : K_CHUNKS * (i + 1)],
+                in_=raw[:].rearrange("p g t -> p (g t)"),
+            )
+        for twice, tab in ((cos_qk, cos_tab), (sin_qk, sin_tab)):
+            nc.vector.tensor_copy(
+                out=twice[:],
+                in_=tab[:]
+                .rearrange("p e s j -> p e (s j)")
+                .unsqueeze(1)
+                .to_broadcast([P, 2, PARITY, ROT]),
+            )
+        statistics(1)
+        prepare_w(0, 0)
+        transpose_x(0)
+        quantise_x(0)
+        prepare_w(0, 1)
+        transpose_x(1)
+        quantise_x(1)
+
+        for c in range(CHUNKS):
+            last = c == CHUNKS - 1
+            for b in range(B):
+                if not last:
+                    prepare_w(c + 1, b)
+                project(c, b)
+                if last:
+                    rotate(nc.vector, c, b, 1)
+                    store_qk(c, b)
+                if b == 0 and c > 0:
+                    for earlier_b in range(B):
+                        store_qk(c - 1, earlier_b)
+            if not last:
+                rotate(nc.gpsimd, c, 0, B)

@@ -27,6 +27,8 @@ CHUNK_HEADS = 2
 CHUNKS = H // CHUNK_HEADS
 CHUNK_BLOCKS = 3 * CHUNK_HEADS
 CHUNK_COLS = CHUNK_BLOCKS * HD
+BLOCKS = 3 * H
+BIAS_BANK = 8
 WIDE_BLOCKS = 4
 WIDE_COLS = WIDE_BLOCKS * HD
 BN_FMAX = 512
@@ -68,7 +70,8 @@ def tile_customgptneoxlayer_pa_kernel(
             [wpool.tile([P, PACK, CHUNK_COLS], BF16, name="wraw%d_%d" % (c, g)) for g in range(PASSES)]
             for c in range(CHUNKS)
         ]
-        bias_bc = [consts.tile([P, CHUNK_BLOCKS, HD], BF16, name="bias_bc%d" % c) for c in range(CHUNKS)]
+        bias_rows = consts.tile([P, P], BF16)
+        bias_bc = consts.tile([P, BLOCKS, HD], BF16)
         wcodes = [
             wpool.tile([P, PASSES, CHUNK_COLS], U32, name="wcodes%d" % c, align_bytes=64)
             for c in range(CHUNKS)
@@ -97,6 +100,10 @@ def tile_customgptneoxlayer_pa_kernel(
                 out=wraw[c][g][:], in_=w_rows[g][:, :, CHUNK_COLS * c : CHUNK_COLS * (c + 1)]
             )
 
+        nc.vector.memset(bias_rows[:], 0.0)
+        b_rows = b_qkv.rearrange("(n d) -> n d", d=HD)
+        for rows in (slice(0, 16), slice(16, BLOCKS)):
+            nc.scalar.dma_start(out=bias_rows[rows, :], in_=b_rows[rows, :])
         load_x(0)
         for raw, param in ((gain_raw, ln1_g), (shift_raw, ln1_b)):
             nc.sync.dma_start(
@@ -105,19 +112,16 @@ def tile_customgptneoxlayer_pa_kernel(
         load_w(0, 0)
         load_x(1)
         load_w(0, 1)
-        for c in range(CHUNKS):
-            nc.sync.dma_start(
-                out=bias_bc[c][:].rearrange("p n d -> p (n d)"),
-                in_=b_qkv[CHUNK_COLS * c : CHUNK_COLS * (c + 1)].partition_broadcast(P),
-            )
-            if c + 1 < CHUNKS:
-                for g in range(PASSES):
-                    load_w(c + 1, g)
+        for c in range(1, CHUNKS):
+            for g in range(PASSES):
+                load_w(c, g)
 
         pos_i = consts.tile([P, PARITY], I32)
         nc.gpsimd.iota(pos_i[:], pattern=[[1, PARITY]], base=0, channel_multiplier=PARITY)
         ident_f32 = consts.tile([P, P], F32)
         make_identity(nc, ident_f32[:])
+        ident_bf16 = consts.tile([P, P], BF16)
+        nc.gpsimd.tensor_copy(out=ident_bf16[:], in_=ident_f32[:])
         neg_half = consts.tile([P, PARITY], F32)
         nc.vector.memset(neg_half[:], -0.5)
 
@@ -259,6 +263,7 @@ def tile_customgptneoxlayer_pa_kernel(
             )
 
         def project(c, b):
+            bias_c = bias_bc[:, CHUNK_BLOCKS * c : CHUNK_BLOCKS * (c + 1), :]
             blocks = res[c][:, b].rearrange("p h w e d -> p (h w) e d")
             n_narrow = CHUNK_BLOCKS - WIDE_BLOCKS
             acc_wide = []
@@ -273,13 +278,13 @@ def tile_customgptneoxlayer_pa_kernel(
                 nc.vector.tensor_tensor(
                     out=blocks[:, 0:WIDE_BLOCKS, e, :],
                     in0=acc_wide[e][:],
-                    in1=bias_bc[c][:, 0:WIDE_BLOCKS, :],
+                    in1=bias_c[:, 0:WIDE_BLOCKS, :],
                     op=ALU.add,
                 )
             nc.vector.tensor_tensor(
                 out=blocks[:, WIDE_BLOCKS:CHUNK_BLOCKS].rearrange("p n e d -> p e n d"),
                 in0=acc_narrow[:],
-                in1=bias_bc[c][:, WIDE_BLOCKS:CHUNK_BLOCKS, :]
+                in1=bias_c[:, WIDE_BLOCKS:CHUNK_BLOCKS, :]
                 .unsqueeze(1)
                 .to_broadcast([P, PARITY, n_narrow, HD]),
                 op=ALU.add,
@@ -314,6 +319,19 @@ def tile_customgptneoxlayer_pa_kernel(
             store(c, b, 0)
             store(c, b, 1)
 
+        bias_t = psum.tile([P, P], BF16, tag="bank")
+        nc.tensor.transpose(bias_t[:], bias_rows[:], ident_bf16[:])
+        bias_cols = consts.tile([P, BLOCKS], BF16)
+        nc.scalar.copy(out=bias_cols[:], in_=bias_t[:, 0:BLOCKS])
+        for first in range(0, BLOCKS, BIAS_BANK):
+            spread = psum.tile([P, BIAS_BANK, HD], BF16, tag="bank")
+            for n in range(BIAS_BANK):
+                nc.tensor.transpose(
+                    spread[:, n, :],
+                    bias_cols[:, first + n : first + n + 1].to_broadcast([P, P]),
+                    ident_bf16[:],
+                )
+            nc.scalar.copy(out=bias_bc[:, first : first + BIAS_BANK, :], in_=spread[:])
         statistics(0)
         for i, raw in enumerate((gain_raw, shift_raw)):
             nc.vector.tensor_copy(

@@ -28,7 +28,6 @@ CHUNKS = H // CHUNK_HEADS
 CHUNK_BLOCKS = 3 * CHUNK_HEADS
 CHUNK_COLS = CHUNK_BLOCKS * HD
 BLOCKS = 3 * H
-BIAS_BANK = 8
 WIDE_BLOCKS = 4
 WIDE_COLS = WIDE_BLOCKS * HD
 BN_FMAX = 512
@@ -234,7 +233,12 @@ def tile_customgptneoxlayer_pa_kernel(
         def prepare_w(c, g):
             wg = stage.tile([P, CHUNK_COLS, PACK], BF16, align_bytes=64, name="wg")
             for part in (wide, narrow):
-                regroup(nc.scalar.copy, wg[:, part, :], wraw[c][g][:, :, part])
+                on_vector = part is narrow and g == 0
+                regroup(
+                    nc.vector.tensor_copy if on_vector else nc.scalar.copy,
+                    wg[:, part, :],
+                    wraw[c][g][:, :, part],
+                )
             for part in (wide, narrow):
                 nc.vector.quantize_mx(
                     out=wcodes[c][:, g, part].bitcast(FP8X4),
@@ -254,6 +258,17 @@ def tile_customgptneoxlayer_pa_kernel(
                     start=(g == 0),
                     stop=(g == PASSES - 1),
                 )
+
+        def spread_bias(c):
+            first = CHUNK_BLOCKS * c
+            spread = psum.tile([P, CHUNK_BLOCKS, HD], BF16, tag="bank")
+            for n in range(CHUNK_BLOCKS):
+                nc.tensor.transpose(
+                    spread[:, n, :],
+                    bias_cols[:, first + n : first + n + 1].to_broadcast([P, P]),
+                    ident_bf16[:],
+                )
+            nc.scalar.copy(out=bias_bc[:, first : first + CHUNK_BLOCKS, :], in_=spread[:])
 
         def store(c, b, w):
             heads = slice(CHUNK_HEADS * c, CHUNK_HEADS * (c + 1))
@@ -320,18 +335,7 @@ def tile_customgptneoxlayer_pa_kernel(
             store(c, b, 1)
 
         bias_t = psum.tile([P, P], BF16, tag="bank")
-        nc.tensor.transpose(bias_t[:], bias_rows[:], ident_bf16[:])
         bias_cols = consts.tile([P, BLOCKS], BF16)
-        nc.scalar.copy(out=bias_cols[:], in_=bias_t[:, 0:BLOCKS])
-        for first in range(0, BLOCKS, BIAS_BANK):
-            spread = psum.tile([P, BIAS_BANK, HD], BF16, tag="bank")
-            for n in range(BIAS_BANK):
-                nc.tensor.transpose(
-                    spread[:, n, :],
-                    bias_cols[:, first + n : first + n + 1].to_broadcast([P, P]),
-                    ident_bf16[:],
-                )
-            nc.scalar.copy(out=bias_bc[:, first : first + BIAS_BANK, :], in_=spread[:])
         statistics(0)
         for i, raw in enumerate((gain_raw, shift_raw)):
             nc.vector.tensor_copy(
@@ -348,9 +352,12 @@ def tile_customgptneoxlayer_pa_kernel(
             )
         statistics(1)
         prepare_w(0, 0)
+        nc.tensor.transpose(bias_t[:], bias_rows[:], ident_bf16[:])
+        nc.scalar.copy(out=bias_cols[:], in_=bias_t[:, 0:BLOCKS])
         transpose_x(0)
         quantise_x(0)
         prepare_w(0, 1)
+        spread_bias(0)
         transpose_x(1)
         quantise_x(1)
 
@@ -359,6 +366,8 @@ def tile_customgptneoxlayer_pa_kernel(
             for b in range(B):
                 if not last:
                     prepare_w(c + 1, b)
+                    if b == B - 1:
+                        spread_bias(c + 1)
                 project(c, b)
                 if last:
                     rotate(nc.vector, c, b, 1)

@@ -233,12 +233,7 @@ def tile_customgptneoxlayer_pa_kernel(
         def prepare_w(c, g):
             wg = stage.tile([P, CHUNK_COLS, PACK], BF16, align_bytes=64, name="wg")
             for part in (wide, narrow):
-                on_vector = part is narrow and g == 0
-                regroup(
-                    nc.vector.tensor_copy if on_vector else nc.scalar.copy,
-                    wg[:, part, :],
-                    wraw[c][g][:, :, part],
-                )
+                regroup(nc.scalar.copy, wg[:, part, :], wraw[c][g][:, :, part])
             for part in (wide, narrow):
                 nc.vector.quantize_mx(
                     out=wcodes[c][:, g, part].bitcast(FP8X4),
@@ -369,11 +364,8 @@ def tile_customgptneoxlayer_pa_kernel(
                     if b == B - 1:
                         spread_bias(c + 1)
                 project(c, b)
+                rotate(nc.vector if last else nc.gpsimd, c, b, 1)
+                if c > 0:
+                    store_qk(c - 1, b)
                 if last:
-                    rotate(nc.vector, c, b, 1)
                     store_qk(c, b)
-                if b == 0 and c > 0:
-                    for earlier_b in range(B):
-                        store_qk(c - 1, earlier_b)
-            if not last:
-                rotate(nc.gpsimd, c, 0, B)

@@ -23,13 +23,15 @@ PACK = 4
 PASSES = D // (P * PACK)
 K_CHUNKS = D // P
 PARITY = S // P
-CHUNK_HEADS = 2
-CHUNKS = H // CHUNK_HEADS
-CHUNK_BLOCKS = 3 * CHUNK_HEADS
-CHUNK_COLS = CHUNK_BLOCKS * HD
-BLOCKS = 3 * H
+HEAD_COLS = 3 * HD
+QK_COLS = 2 * HD
+PAIRS = 3
+SINGLES = (6, 7)
+UNIT_COLS = 2 * HEAD_COLS
+UNITS = 2 * PAIRS + len(SINGLES)
 WIDE_BLOCKS = 4
 WIDE_COLS = WIDE_BLOCKS * HD
+BLOCKS = 3 * H
 BN_FMAX = 512
 BN_STATS_DIM = 6
 ROUND_MAGIC = 1.5 * 2.0**23
@@ -49,13 +51,11 @@ def tile_customgptneoxlayer_pa_kernel(
 ):
     nc = tc.nc
     outs = (out_0, out_1, out_2)
-    wide = slice(0, WIDE_COLS)
-    narrow = slice(WIDE_COLS, CHUNK_COLS)
     with ExitStack() as stack:
         consts = stack.enter_context(tc.tile_pool(name="consts", bufs=1))
         xpool = stack.enter_context(tc.tile_pool(name="xpool", bufs=1))
         wpool = stack.enter_context(tc.tile_pool(name="wpool", bufs=1))
-        stage = stack.enter_context(tc.tile_pool(name="stage", bufs=3))
+        stage = stack.enter_context(tc.tile_pool(name="stage", bufs=4))
         respool = stack.enter_context(tc.tile_pool(name="respool", bufs=1))
         ropepool = stack.enter_context(tc.tile_pool(name="ropepool", bufs=2))
         psum = stack.enter_context(tc.psum_pool(name="psum", bufs=8))
@@ -63,64 +63,51 @@ def tile_customgptneoxlayer_pa_kernel(
 
         gain_raw = consts.tile([P, PASSES, PACK], BF16)
         shift_raw = consts.tile([P, PASSES, PACK], BF16)
+        bias_bc = consts.tile([P, BLOCKS, HD], BF16)
         x_sb = [xpool.tile([P, PARITY, D], BF16, name="x_sb%d" % b) for b in range(B)]
         xn = [xpool.tile([P, PARITY, D], F32, name="xn%d" % b) for b in range(B)]
-        wraw = [
-            [wpool.tile([P, PACK, CHUNK_COLS], BF16, name="wraw%d_%d" % (c, g)) for g in range(PASSES)]
-            for c in range(CHUNKS)
-        ]
-        bias_rows = consts.tile([P, P], BF16)
-        bias_bc = consts.tile([P, BLOCKS, HD], BF16)
-        wcodes = [
-            wpool.tile([P, PASSES, CHUNK_COLS], U32, name="wcodes%d" % c, align_bytes=64)
-            for c in range(CHUNKS)
-        ]
-        wscales = [
-            wpool.tile([P, PASSES, CHUNK_COLS], U8, name="wscales%d" % c, align_bytes=64)
-            for c in range(CHUNKS)
-        ]
         xb = xpool.tile([P, B, K_CHUNKS, S], BF16)
         xcodes = xpool.tile([P, B, PASSES, S], U32, align_bytes=64)
         xscales = xpool.tile([P, B, PASSES, S], U8, align_bytes=64)
+        w_codes = [wpool.tile([P, UNIT_COLS], U32, name="w_codes%d" % u, align_bytes=64) for u in range(UNITS)]
+        w_scales = [wpool.tile([P, UNIT_COLS], U8, name="w_scales%d" % u, align_bytes=64) for u in range(UNITS)]
         res = [
-            respool.tile([P, B, CHUNK_HEADS, 3, PARITY, HD], F32, name="res%d" % c)
-            for c in range(CHUNKS)
+            respool.tile([P, B, 2 if i < PAIRS else 1, 3, PARITY, HD], F32, name="res%d" % i)
+            for i in range(PAIRS + len(SINGLES))
         ]
 
-        def load_x(b):
+        def load_x(b, *parities):
             rows = hidden_states[b].rearrange("(p e) d -> p e d", e=PARITY)
-            for e in range(PARITY):
+            for e in parities or range(PARITY):
                 nc.sync.dma_start(out=x_sb[b][:, e, :], in_=rows[:, e, :])
 
         w_rows = W_qkv.rearrange("(g p t) n -> g p t n", t=PACK, p=P)
+        wraw = {}
 
-        def load_w(c, g):
-            nc.sync.dma_start(
-                out=wraw[c][g][:], in_=w_rows[g][:, :, CHUNK_COLS * c : CHUNK_COLS * (c + 1)]
-            )
+        def load_w(pair, g):
+            tile = wpool.tile([P, PACK, UNIT_COLS], BF16, name="wraw%d_%d" % (pair, g))
+            cols = slice(UNIT_COLS * pair, UNIT_COLS * (pair + 1))
+            nc.sync.dma_start(out=tile[:], in_=w_rows[g][:, :, cols])
+            wraw[pair, g] = tile
 
-        nc.vector.memset(bias_rows[:], 0.0)
-        b_rows = b_qkv.rearrange("(n d) -> n d", d=HD)
-        for rows in (slice(0, 16), slice(16, BLOCKS)):
-            nc.scalar.dma_start(out=bias_rows[rows, :], in_=b_rows[rows, :])
         load_x(0)
         for raw, param in ((gain_raw, ln1_g), (shift_raw, ln1_b)):
-            nc.sync.dma_start(
-                out=raw[:], in_=param.rearrange("(g p t) -> p g t", t=PACK, p=P)
-            )
+            nc.sync.dma_start(out=raw[:], in_=param.rearrange("(g p t) -> p g t", t=PACK, p=P))
         load_w(0, 0)
         load_x(1)
         load_w(0, 1)
-        for c in range(1, CHUNKS):
+        for pair in range(1, H // 2):
             for g in range(PASSES):
-                load_w(c, g)
+                load_w(pair, g)
+                if (pair, g) == (1, 0):
+                    nc.sync.dma_start(
+                        out=bias_bc[:].rearrange("p n d -> p (n d)"), in_=b_qkv.partition_broadcast(P)
+                    )
 
         pos_i = consts.tile([P, PARITY], I32)
         nc.gpsimd.iota(pos_i[:], pattern=[[1, PARITY]], base=0, channel_multiplier=PARITY)
         ident_f32 = consts.tile([P, P], F32)
         make_identity(nc, ident_f32[:])
-        ident_bf16 = consts.tile([P, P], BF16)
-        nc.gpsimd.tensor_copy(out=ident_bf16[:], in_=ident_f32[:])
         neg_half = consts.tile([P, PARITY], F32)
         nc.vector.memset(neg_half[:], -0.5)
 
@@ -167,7 +154,7 @@ def tile_customgptneoxlayer_pa_kernel(
         sin_qk = consts.tile([P, 2, PARITY, ROT], F32)
         gb_cols = consts.tile([P, 2 * K_CHUNKS], F32)
 
-        def statistics(b):
+        def normalise(b, engine=nc.gpsimd):
             stats = xpool.tile([P, PARITY, D // BN_FMAX, BN_STATS_DIM], F32, name="stats%d" % b)
             mean_var = xpool.tile([P, PARITY, 2], F32, name="mean_var%d" % b)
             for e in range(PARITY):
@@ -189,7 +176,7 @@ def tile_customgptneoxlayer_pa_kernel(
             rstd = xpool.tile([P, PARITY], F32, name="rstd%d" % b)
             nc.gpsimd.tensor_tensor(out=rstd[:], in0=var_eps[:], in1=neg_half[:], op=ALU.pow)
             for e in range(PARITY):
-                nc.gpsimd.tensor_scalar(
+                engine.tensor_scalar(
                     out=xn[b][:, e, :].rearrange("p (g t q) -> p g t q", g=PASSES, t=PACK),
                     in0=x_sb[b][:, e, :].rearrange("p (g q t) -> p g t q", g=PASSES, t=PACK),
                     scalar1=neg_mean[:, e : e + 1],
@@ -211,161 +198,253 @@ def tile_customgptneoxlayer_pa_kernel(
                         )
                 for ai in range(2):
                     a = 2 * i + ai
+                    gain = gb_cols[:, a : a + 1]
+                    shift = gb_cols[:, K_CHUNKS + a : K_CHUNKS + a + 1]
                     nc.vector.tensor_scalar(
                         out=xb[:, b, a, :],
                         in0=xt[:, ai, :],
-                        scalar1=gb_cols[:, a : a + 1],
-                        scalar2=gb_cols[:, K_CHUNKS + a : K_CHUNKS + a + 1],
+                        scalar1=gain,
+                        scalar2=shift,
                         op0=ALU.mult,
                         op1=ALU.add,
                     )
 
+        xgroups = {}
+
+        def regroup_x(b):
+            xgroups[b] = xpool.tile([P, PASSES, S, PACK], BF16, name="xg%d" % b, align_bytes=64)
+            nc.vector.tensor_copy(
+                out=xgroups[b][:].rearrange("p g (c i) t -> p g c t i", i=4),
+                in_=xb[:, b].rearrange("p (g t) (c i) -> p g c t i", t=PACK, i=4),
+            )
+
         def quantise_x(b):
-            xg = xpool.tile([P, PASSES, S, PACK], BF16, name="xg%d" % b, align_bytes=64)
-            for g in range(PASSES):
-                regroup(nc.vector.tensor_copy, xg[:, g], xb[:, b, PACK * g : PACK * (g + 1), :])
             nc.vector.quantize_mx(
                 out=xcodes[:, b].rearrange("p g c -> p (g c)").bitcast(FP8X4),
                 scales=xscales[:, b].rearrange("p g c -> p (g c)"),
-                in_=xg[:].rearrange("p g c t -> p (g c t)"),
+                in_=xgroups[b][:].rearrange("p g c t -> p (g c t)"),
             )
 
-        def prepare_w(c, g):
-            wg = stage.tile([P, CHUNK_COLS, PACK], BF16, align_bytes=64, name="wg")
-            for part in (wide, narrow):
-                regroup(nc.scalar.copy, wg[:, part, :], wraw[c][g][:, :, part])
-            for part in (wide, narrow):
+        wgroups = {}
+
+        def regroup_w(u):
+            wgroups[u] = stage.tile([P, UNIT_COLS, PACK], BF16, align_bytes=64, name="wg")
+            if u < 2 * PAIRS:
+                regroup(nc.scalar.copy, wgroups[u][:], wraw[u // 2, u % 2][:])
+            else:
+                h = SINGLES[u - 2 * PAIRS]
+                cols = slice(HEAD_COLS * (h % 2), HEAD_COLS * (h % 2 + 1))
+                for g in range(PASSES):
+                    regroup(nc.scalar.copy, wgroups[u][:, HEAD_COLS * g : HEAD_COLS * (g + 1), :], wraw[h // 2, g][:, :, cols])
+
+        def quantise_w(u):
+            for cols in (slice(0, 512), slice(512, 768)):
                 nc.vector.quantize_mx(
-                    out=wcodes[c][:, g, part].bitcast(FP8X4),
-                    scales=wscales[c][:, g, part],
-                    in_=wg[:, part, :].rearrange("p c t -> p (c t)"),
+                    out=w_codes[u][:, cols].bitcast(FP8X4),
+                    scales=w_scales[u][:, cols],
+                    in_=wgroups[u][:, cols, :].rearrange("p c t -> p (c t)"),
                 )
 
-        def mx_group(acc, b, e, c, part):
+        def mx_group(acc, b, e, operands):
             tokens = slice(P * e, P * (e + 1))
-            for g in range(PASSES):
+            for g, (u, cols) in enumerate(operands):
                 nc.tensor.matmul_mx(
                     out=acc,
                     lhsT=xcodes[:, b, g, tokens].bitcast(FP8X4),
                     lhsT_scale=xscales[:, b, g, tokens],
-                    rhs=wcodes[c][:, g, part].bitcast(FP8X4),
-                    rhs_scale=wscales[c][:, g, part],
+                    rhs=w_codes[u][:, cols].bitcast(FP8X4),
+                    rhs_scale=w_scales[u][:, cols],
                     start=(g == 0),
                     stop=(g == PASSES - 1),
                 )
 
-        def spread_bias(c):
-            first = CHUNK_BLOCKS * c
-            spread = psum.tile([P, CHUNK_BLOCKS, HD], BF16, tag="bank")
-            for n in range(CHUNK_BLOCKS):
-                nc.tensor.transpose(
-                    spread[:, n, :],
-                    bias_cols[:, first + n : first + n + 1].to_broadcast([P, P]),
-                    ident_bf16[:],
+        def store(i, w, batches=slice(0, B)):
+            if i < PAIRS:
+                for b in range(batches.start, batches.stop):
+                    nc.sync.dma_start(
+                        out=outs[w][b, 2 * i : 2 * i + 2].rearrange("h (p e) d -> p h (e d)", e=PARITY),
+                        in_=res[i][:, b, :, w].rearrange("p h e d -> p h (e d)"),
+                    )
+            else:
+                nc.sync.dma_start(
+                    out=outs[w][batches, SINGLES[i - PAIRS]].rearrange("b (p e) d -> p b (e d)", e=PARITY),
+                    in_=res[i][:, batches, 0, w].rearrange("p b e d -> p b (e d)"),
                 )
-            nc.scalar.copy(out=bias_bc[:, first : first + CHUNK_BLOCKS, :], in_=spread[:])
 
-        def store(c, b, w):
-            heads = slice(CHUNK_HEADS * c, CHUNK_HEADS * (c + 1))
-            nc.sync.dma_start(
-                out=outs[w][b, heads].rearrange("h (p e) d -> p h (e d)", e=PARITY),
-                in_=res[c][:, b, :, w].rearrange("p h e d -> p h (e d)"),
-            )
+        def store_qk(i, batches=slice(0, B)):
+            store(i, 0, batches)
+            store(i, 1, batches)
 
-        def project(c, b):
-            bias_c = bias_bc[:, CHUNK_BLOCKS * c : CHUNK_BLOCKS * (c + 1), :]
-            blocks = res[c][:, b].rearrange("p h w e d -> p (h w) e d")
-            n_narrow = CHUNK_BLOCKS - WIDE_BLOCKS
+        accs = {}
+
+        def multiply_pair(i, b):
             acc_wide = []
             for e in range(PARITY):
                 acc = psum.tile([P, WIDE_BLOCKS, HD], F32, tag="bank", name="acc_wide%d" % e)
-                mx_group(acc[:].rearrange("p n d -> p (n d)"), b, e, c, wide)
+                operands = [(2 * i + g, slice(0, WIDE_COLS)) for g in range(PASSES)]
+                mx_group(acc[:].rearrange("p n d -> p (n d)"), b, e, operands)
                 acc_wide.append(acc)
-            acc_narrow = psum.tile([P, PARITY, n_narrow, HD], F32, tag="bank")
+            acc_narrow = psum.tile([P, PARITY, 2, HD], F32, tag="bank", name="acc_narrow")
             for e in range(PARITY):
-                mx_group(acc_narrow[:, e].rearrange("p n d -> p (n d)"), b, e, c, narrow)
+                operands = [(2 * i + g, slice(WIDE_COLS, UNIT_COLS)) for g in range(PASSES)]
+                mx_group(acc_narrow[:, e].rearrange("p n d -> p (n d)"), b, e, operands)
+            accs[i, b] = acc_wide, acc_narrow
+
+        def leave_pair(i, b):
+            acc_wide, acc_narrow = accs[i, b]
+            first = 6 * i
+            blocks = res[i][:, b].rearrange("p h w e d -> p (h w) e d")
             for e in range(PARITY):
                 nc.vector.tensor_tensor(
                     out=blocks[:, 0:WIDE_BLOCKS, e, :],
                     in0=acc_wide[e][:],
-                    in1=bias_c[:, 0:WIDE_BLOCKS, :],
+                    in1=bias_bc[:, first : first + WIDE_BLOCKS, :],
                     op=ALU.add,
                 )
             nc.vector.tensor_tensor(
-                out=blocks[:, WIDE_BLOCKS:CHUNK_BLOCKS].rearrange("p n e d -> p e n d"),
+                out=blocks[:, WIDE_BLOCKS:6].rearrange("p n e d -> p e n d"),
                 in0=acc_narrow[:],
-                in1=bias_c[:, WIDE_BLOCKS:CHUNK_BLOCKS, :]
+                in1=bias_bc[:, first + WIDE_BLOCKS : first + 6, :]
                 .unsqueeze(1)
-                .to_broadcast([P, PARITY, n_narrow, HD]),
+                .to_broadcast([P, PARITY, 2, HD]),
                 op=ALU.add,
             )
-            store(c, b, 2)
+            store(i, 2, slice(b, b + 1))
 
-        def rotate(engine, c, first_b, n_b):
-            u = res[c][:, first_b : first_b + n_b, :, 0:2, :, 0:ROT].rearrange(
-                "p b h w e j -> p (b h) (w e) j"
+        def multiply_single(i):
+            u = PAIRS + i
+            for b in range(B):
+                bank = psum.tile([P, PARITY, 2, HD], F32, tag="bank", name="acc_qk")
+                operands = [(u, slice(HEAD_COLS * g, HEAD_COLS * g + QK_COLS)) for g in range(PASSES)]
+                for e in range(PARITY):
+                    mx_group(bank[:, e].rearrange("p n d -> p (n d)"), b, e, operands)
+                accs[i, b] = bank
+            bank = psum.tile([P, B, PARITY, HD], F32, tag="bank", name="acc_val")
+            operands = [(u, slice(HEAD_COLS * g + QK_COLS, HEAD_COLS * (g + 1))) for g in range(PASSES)]
+            for b in range(B):
+                for e in range(PARITY):
+                    mx_group(bank[:, b, e], b, e, operands)
+            accs[i, "val"] = bank
+
+        def leave_qk(i, b):
+            first = 3 * SINGLES[i - PAIRS]
+            nc.vector.tensor_tensor(
+                out=res[i][:, b, 0, 0:2].rearrange("p w e d -> p e w d"),
+                in0=accs[i, b][:],
+                in1=bias_bc[:, first : first + 2, :].unsqueeze(1).to_broadcast([P, PARITY, 2, HD]),
+                op=ALU.add,
             )
-            shape = [P, n_b * CHUNK_HEADS, 2 * PARITY, ROT]
+
+        def leave_val(i):
+            first = 3 * SINGLES[i - PAIRS] + 2
+            nc.vector.tensor_tensor(
+                out=res[i][:, :, 0, 2],
+                in0=accs[i, "val"][:],
+                in1=bias_bc[:, first : first + 1, :].unsqueeze(1).to_broadcast([P, B, PARITY, HD]),
+                op=ALU.add,
+            )
+            store(i, 2)
+
+        def rotate(engine, i, batches=slice(0, B)):
+            u = res[i][:, batches, :, 0:2, :, 0:ROT].rearrange("p b h w e j -> p (b h) (w e) j")
+            shape = list(u.shape)
             cos_b = cos_qk[:].rearrange("p w e j -> p (w e) j").unsqueeze(1).to_broadcast(shape)
             sin_b = sin_qk[:].rearrange("p w e j -> p (w e) j").unsqueeze(1).to_broadcast(shape)
-            straight = ropepool.tile(shape, F32, tag="straight")
-            crossed = ropepool.tile(shape, F32, tag="crossed")
+            who = "v" if engine is nc.vector else "g"
+            straight = ropepool.tile(shape, F32, name="straight_%s%d" % (who, shape[1]))
+            crossed = ropepool.tile(shape, F32, name="crossed_%s%d" % (who, shape[1]))
             engine.tensor_tensor(out=straight[:], in0=u, in1=cos_b, op=ALU.mult)
-            engine.tensor_tensor(
-                out=crossed[:, :, :, 0:HALF],
-                in0=u[:, :, :, HALF:ROT],
-                in1=sin_b[:, :, :, 0:HALF],
-                op=ALU.mult,
-            )
-            engine.tensor_tensor(
-                out=crossed[:, :, :, HALF:ROT],
-                in0=u[:, :, :, 0:HALF],
-                in1=sin_b[:, :, :, HALF:ROT],
-                op=ALU.mult,
-            )
+            if shape[1] == 1:
+                swapped = u.rearrange("p a c (z j) -> p a c z j", z=2)[:, :, :, ::-1, :]
+                engine.tensor_tensor(
+                    out=crossed[:].rearrange("p a c (z j) -> p a c z j", z=2),
+                    in0=swapped,
+                    in1=sin_b.rearrange("p a c (z j) -> p a c z j", z=2),
+                    op=ALU.mult,
+                )
+            else:
+                engine.tensor_tensor(
+                    out=crossed[:, :, :, 0:HALF],
+                    in0=u[:, :, :, HALF:ROT],
+                    in1=sin_b[:, :, :, 0:HALF],
+                    op=ALU.mult,
+                )
+                engine.tensor_tensor(
+                    out=crossed[:, :, :, HALF:ROT],
+                    in0=u[:, :, :, 0:HALF],
+                    in1=sin_b[:, :, :, HALF:ROT],
+                    op=ALU.mult,
+                )
             engine.tensor_tensor(out=u, in0=straight[:], in1=crossed[:], op=ALU.add)
 
-        def store_qk(c, b):
-            store(c, b, 0)
-            store(c, b, 1)
+        def gain_and_shift():
+            for i, raw in enumerate((gain_raw, shift_raw)):
+                nc.vector.tensor_copy(
+                    out=gb_cols[:, K_CHUNKS * i : K_CHUNKS * (i + 1)],
+                    in_=raw[:].rearrange("p g t -> p (g t)"),
+                )
 
-        bias_t = psum.tile([P, P], BF16, tag="bank")
-        bias_cols = consts.tile([P, BLOCKS], BF16)
-        statistics(0)
-        for i, raw in enumerate((gain_raw, shift_raw)):
-            nc.vector.tensor_copy(
-                out=gb_cols[:, K_CHUNKS * i : K_CHUNKS * (i + 1)],
-                in_=raw[:].rearrange("p g t -> p (g t)"),
-            )
-        for twice, tab in ((cos_qk, cos_tab), (sin_qk, sin_tab)):
-            nc.vector.tensor_copy(
-                out=twice[:],
-                in_=tab[:]
-                .rearrange("p e s j -> p e (s j)")
-                .unsqueeze(1)
-                .to_broadcast([P, 2, PARITY, ROT]),
-            )
-        statistics(1)
-        prepare_w(0, 0)
-        nc.tensor.transpose(bias_t[:], bias_rows[:], ident_bf16[:])
-        nc.scalar.copy(out=bias_cols[:], in_=bias_t[:, 0:BLOCKS])
+        def double_tables():
+            for twice, tab in ((cos_qk, cos_tab), (sin_qk, sin_tab)):
+                nc.vector.tensor_copy(
+                    out=twice[:],
+                    in_=tab[:]
+                    .rearrange("p e s j -> p e (s j)")
+                    .unsqueeze(1)
+                    .to_broadcast([P, 2, PARITY, ROT]),
+                )
+
+        normalise(0)
+        gain_and_shift()
+        double_tables()
+
+        normalise(1)
+
+        regroup_w(0)
+        quantise_w(0)
+
         transpose_x(0)
+
+        regroup_x(0)
         quantise_x(0)
-        prepare_w(0, 1)
-        spread_bias(0)
+        regroup_w(1)
+        quantise_w(1)
+
+
         transpose_x(1)
+
+        regroup_x(1)
         quantise_x(1)
 
-        for c in range(CHUNKS):
-            last = c == CHUNKS - 1
+        for i in range(PAIRS):
             for b in range(B):
-                if not last:
-                    prepare_w(c + 1, b)
-                    if b == B - 1:
-                        spread_bias(c + 1)
-                project(c, b)
-                rotate(nc.vector if last else nc.gpsimd, c, b, 1)
-                if c > 0:
-                    store_qk(c - 1, b)
-                if last:
-                    store_qk(c, b)
+                n = B * i + b
+                if n + 2 < UNITS:
+                    regroup_w(n + 2)
+                    if n + 3 < UNITS:
+                        quantise_w(n + 2)
+                multiply_pair(i, b)
+
+                leave_pair(i, b)
+                on_vector = n not in range(5)
+                batch = slice(b, b + 1)
+                rotate(nc.vector if on_vector else nc.gpsimd, i, batch)
+                if on_vector:
+                    store_qk(i, batch)
+                if n - 2 in range(5):
+                    store_qk((n - 2) // B, slice((n - 2) % B, (n - 2) % B + 1))
+        quantise_w(7)
+        multiply_single(PAIRS)
+        multiply_single(PAIRS + 1)
+        for i in (PAIRS, PAIRS + 1):
+            leave_qk(i, 0)
+            leave_qk(i, 1)
+            for b in range(B):
+                batch = slice(b, b + 1)
+                rotate(nc.vector, i, batch)
+                store_qk(i, batch)
+                if b == 0:
+                    leave_val(i)
+                n = 6 + (i - PAIRS) * B + b
+                if n - 2 in range(5) and n - 2 < 6:
+                    store_qk((n - 2) // B, slice((n - 2) % B, (n - 2) % B + 1))

@@ -91,10 +91,10 @@ def tile_customgptneoxlayer_pa_kernel(
             wraw[pair, g] = tile
 
         load_x(0)
-        for raw, param in ((gain_raw, ln1_g), (shift_raw, ln1_b)):
-            nc.sync.dma_start(out=raw[:], in_=param.rearrange("(g p t) -> p g t", t=PACK, p=P))
         load_w(0, 0)
         load_x(1)
+        for raw, param in ((gain_raw, ln1_g), (shift_raw, ln1_b)):
+            nc.sync.dma_start(out=raw[:], in_=param.rearrange("(g p t) -> p g t", t=PACK, p=P))
         load_w(0, 1)
         for pair in range(1, H // 2):
             for g in range(PASSES):
@@ -154,17 +154,28 @@ def tile_customgptneoxlayer_pa_kernel(
         sin_qk = consts.tile([P, 2, PARITY, ROT], F32)
         gb_cols = consts.tile([P, 2 * K_CHUNKS], F32)
 
-        def normalise(b, engine=nc.gpsimd):
+        def normalise(b, fillers):
             stats = xpool.tile([P, PARITY, D // BN_FMAX, BN_STATS_DIM], F32, name="stats%d" % b)
             mean_var = xpool.tile([P, PARITY, 2], F32, name="mean_var%d" % b)
-            for e in range(PARITY):
-                for f in range(D // BN_FMAX):
-                    nc.vector.bn_stats(
-                        out=stats[:, e, f, :], in_=x_sb[b][:, e, BN_FMAX * f : BN_FMAX * (f + 1)]
-                    )
+
+            def partial(e, f):
+                nc.vector.bn_stats(
+                    out=stats[:, e, f, :], in_=x_sb[b][:, e, BN_FMAX * f : BN_FMAX * (f + 1)]
+                )
+
+            def aggregate(e):
                 nc.vector.bn_aggr(
                     out=mean_var[:, e, :], in_=stats[:, e].rearrange("p f s -> p (f s)")
                 )
+
+            partial(0, 0)
+            partial(0, 1)
+            partial(1, 0)
+            aggregate(0)
+            partial(1, 1)
+            fillers[0]()
+            aggregate(1)
+            fillers[1]()
             neg_mean = xpool.tile([P, PARITY], F32, name="neg_mean%d" % b)
             nc.vector.tensor_scalar(
                 out=neg_mean[:], in0=mean_var[:, :, 0], scalar1=-1.0, scalar2=None, op0=ALU.mult
@@ -176,7 +187,7 @@ def tile_customgptneoxlayer_pa_kernel(
             rstd = xpool.tile([P, PARITY], F32, name="rstd%d" % b)
             nc.gpsimd.tensor_tensor(out=rstd[:], in0=var_eps[:], in1=neg_half[:], op=ALU.pow)
             for e in range(PARITY):
-                engine.tensor_scalar(
+                nc.gpsimd.tensor_scalar(
                     out=xn[b][:, e, :].rearrange("p (g t q) -> p g t q", g=PASSES, t=PACK),
                     in0=x_sb[b][:, e, :].rearrange("p (g q t) -> p g t q", g=PASSES, t=PACK),
                     scalar1=neg_mean[:, e : e + 1],
@@ -237,8 +248,8 @@ def tile_customgptneoxlayer_pa_kernel(
                 for g in range(PASSES):
                     regroup(nc.scalar.copy, wgroups[u][:, HEAD_COLS * g : HEAD_COLS * (g + 1), :], wraw[h // 2, g][:, :, cols])
 
-        def quantise_w(u):
-            for cols in (slice(0, 512), slice(512, 768)):
+        def quantise_w(u, pieces=(slice(0, 512), slice(512, 768))):
+            for cols in pieces:
                 nc.vector.quantize_mx(
                     out=w_codes[u][:, cols].bitcast(FP8X4),
                     scales=w_scales[u][:, cols],
@@ -291,6 +302,10 @@ def tile_customgptneoxlayer_pa_kernel(
             accs[i, b] = acc_wide, acc_narrow
 
         def leave_pair(i, b):
+            leave_wide(i, b)
+            leave_narrow(i, b)
+
+        def leave_wide(i, b):
             acc_wide, acc_narrow = accs[i, b]
             first = 6 * i
             blocks = res[i][:, b].rearrange("p h w e d -> p (h w) e d")
@@ -301,6 +316,11 @@ def tile_customgptneoxlayer_pa_kernel(
                     in1=bias_bc[:, first : first + WIDE_BLOCKS, :],
                     op=ALU.add,
                 )
+
+        def leave_narrow(i, b):
+            acc_wide, acc_narrow = accs[i, b]
+            first = 6 * i
+            blocks = res[i][:, b].rearrange("p h w e d -> p (h w) e d")
             nc.vector.tensor_tensor(
                 out=blocks[:, WIDE_BLOCKS:6].rearrange("p n e d -> p e n d"),
                 in0=acc_narrow[:],
@@ -345,106 +365,122 @@ def tile_customgptneoxlayer_pa_kernel(
             )
             store(i, 2)
 
-        def rotate(engine, i, batches=slice(0, B)):
-            u = res[i][:, batches, :, 0:2, :, 0:ROT].rearrange("p b h w e j -> p (b h) (w e) j")
+        def rotation(engine, i, b):
+            u = res[i][:, b : b + 1, :, 0:2, :, 0:ROT].rearrange("p b h w e j -> p (b h) (w e) j")
             shape = list(u.shape)
             cos_b = cos_qk[:].rearrange("p w e j -> p (w e) j").unsqueeze(1).to_broadcast(shape)
             sin_b = sin_qk[:].rearrange("p w e j -> p (w e) j").unsqueeze(1).to_broadcast(shape)
             who = "v" if engine is nc.vector else "g"
             straight = ropepool.tile(shape, F32, name="straight_%s%d" % (who, shape[1]))
             crossed = ropepool.tile(shape, F32, name="crossed_%s%d" % (who, shape[1]))
-            engine.tensor_tensor(out=straight[:], in0=u, in1=cos_b, op=ALU.mult)
-            if shape[1] == 1:
-                swapped = u.rearrange("p a c (z j) -> p a c z j", z=2)[:, :, :, ::-1, :]
-                engine.tensor_tensor(
-                    out=crossed[:].rearrange("p a c (z j) -> p a c z j", z=2),
-                    in0=swapped,
-                    in1=sin_b.rearrange("p a c (z j) -> p a c z j", z=2),
-                    op=ALU.mult,
-                )
-            else:
-                engine.tensor_tensor(
-                    out=crossed[:, :, :, 0:HALF],
-                    in0=u[:, :, :, HALF:ROT],
-                    in1=sin_b[:, :, :, 0:HALF],
-                    op=ALU.mult,
-                )
-                engine.tensor_tensor(
-                    out=crossed[:, :, :, HALF:ROT],
-                    in0=u[:, :, :, 0:HALF],
-                    in1=sin_b[:, :, :, HALF:ROT],
-                    op=ALU.mult,
-                )
-            engine.tensor_tensor(out=u, in0=straight[:], in1=crossed[:], op=ALU.add)
 
-        def gain_and_shift():
-            for i, raw in enumerate((gain_raw, shift_raw)):
-                nc.vector.tensor_copy(
-                    out=gb_cols[:, K_CHUNKS * i : K_CHUNKS * (i + 1)],
-                    in_=raw[:].rearrange("p g t -> p (g t)"),
-                )
+            def first():
+                engine.tensor_tensor(out=straight[:], in0=u, in1=cos_b, op=ALU.mult)
 
-        def double_tables():
-            for twice, tab in ((cos_qk, cos_tab), (sin_qk, sin_tab)):
-                nc.vector.tensor_copy(
-                    out=twice[:],
-                    in_=tab[:]
-                    .rearrange("p e s j -> p e (s j)")
-                    .unsqueeze(1)
-                    .to_broadcast([P, 2, PARITY, ROT]),
-                )
+            def second():
+                if shape[1] == 1:
+                    swapped = u.rearrange("p a c (z j) -> p a c z j", z=2)[:, :, :, ::-1, :]
+                    engine.tensor_tensor(
+                        out=crossed[:].rearrange("p a c (z j) -> p a c z j", z=2),
+                        in0=swapped,
+                        in1=sin_b.rearrange("p a c (z j) -> p a c z j", z=2),
+                        op=ALU.mult,
+                    )
+                    return
+                for to, of in ((slice(0, HALF), slice(HALF, ROT)), (slice(HALF, ROT), slice(0, HALF))):
+                    engine.tensor_tensor(
+                        out=crossed[:, :, :, to],
+                        in0=u[:, :, :, of],
+                        in1=sin_b[:, :, :, to],
+                        op=ALU.mult,
+                    )
 
-        normalise(0)
-        gain_and_shift()
-        double_tables()
+            def third():
+                engine.tensor_tensor(out=u, in0=straight[:], in1=crossed[:], op=ALU.add)
 
-        normalise(1)
+            return first, second, third
 
+        def columns(i, raw):
+            nc.vector.tensor_copy(
+                out=gb_cols[:, K_CHUNKS * i : K_CHUNKS * (i + 1)],
+                in_=raw[:].rearrange("p g t -> p (g t)"),
+            )
+
+        def double(twice, tab):
+            nc.vector.tensor_copy(
+                out=twice[:],
+                in_=tab[:]
+                .rearrange("p e s j -> p e (s j)")
+                .unsqueeze(1)
+                .to_broadcast([P, 2, PARITY, ROT]),
+            )
+
+        wide, narrow = slice(0, 512), slice(512, 768)
+
+        def rotate_gpsimd(n):
+            for step in rotation(nc.gpsimd, n // B, n % B):
+                step()
+
+        def late_store(n):
+            if 0 <= n < 5:
+                store_qk(n // B, slice(n % B, n % B + 1))
+
+        normalise(0, (lambda: double(cos_qk, cos_tab), lambda: double(sin_qk, sin_tab)))
+        normalise(1, (lambda: columns(0, gain_raw), lambda: columns(1, shift_raw)))
         regroup_w(0)
         quantise_w(0)
-
         transpose_x(0)
-
-        regroup_x(0)
-        quantise_x(0)
         regroup_w(1)
-        quantise_w(1)
-
-
+        quantise_w(1, (narrow,))
+        regroup_x(0)
+        quantise_w(1, (wide,))
+        quantise_x(0)
         transpose_x(1)
-
+        multiply_pair(0, 0)
+        leave_wide(0, 0)
         regroup_x(1)
+        leave_narrow(0, 0)
+        rotate_gpsimd(0)
+        regroup_w(2)
         quantise_x(1)
+        quantise_w(2)
+        multiply_pair(0, 1)
+        regroup_w(3)
+        quantise_w(3)
+        leave_pair(0, 1)
+        rotate_gpsimd(1)
 
-        for i in range(PAIRS):
-            for b in range(B):
-                n = B * i + b
-                if n + 2 < UNITS:
-                    regroup_w(n + 2)
-                    if n + 3 < UNITS:
-                        quantise_w(n + 2)
-                multiply_pair(i, b)
-
-                leave_pair(i, b)
-                on_vector = n not in range(5)
-                batch = slice(b, b + 1)
-                rotate(nc.vector if on_vector else nc.gpsimd, i, batch)
-                if on_vector:
-                    store_qk(i, batch)
-                if n - 2 in range(5):
-                    store_qk((n - 2) // B, slice((n - 2) % B, (n - 2) % B + 1))
-        quantise_w(7)
+        for n in range(2, B * PAIRS - 1):
+            i, b = divmod(n, B)
+            regroup_w(n + 2)
+            quantise_w(n + 2)
+            multiply_pair(i, b)
+            leave_pair(i, b)
+            rotate_gpsimd(n)
+            late_store(n - 2)
+        regroup_w(7)
+        multiply_pair(2, 1)
         multiply_single(PAIRS)
+        leave_pair(2, 1)
+        quantise_w(7, (wide,))
+        first, second, third = rotation(nc.vector, 2, 1)
+        first()
+        second()
+        quantise_w(7, (narrow,))
+        third()
+        store_qk(2, slice(1, 2))
         multiply_single(PAIRS + 1)
+        late_store(3)
         for i in (PAIRS, PAIRS + 1):
             leave_qk(i, 0)
             leave_qk(i, 1)
+            steps = [rotation(nc.vector, i, b) for b in range(B)]
+            for step in range(2):
+                for b in range(B):
+                    steps[b][step]()
+            leave_val(i)
             for b in range(B):
-                batch = slice(b, b + 1)
-                rotate(nc.vector, i, batch)
-                store_qk(i, batch)
-                if b == 0:
-                    leave_val(i)
-                n = 6 + (i - PAIRS) * B + b
-                if n - 2 in range(5) and n - 2 < 6:
-                    store_qk((n - 2) // B, slice((n - 2) % B, (n - 2) % B + 1))
+                steps[b][2]()
+                store_qk(i, slice(b, b + 1))
+            if i == PAIRS:
+                late_store(4)

import math
from contextlib import ExitStack

import concourse.mybir as mybir
from concourse.masks import make_identity

F32 = mybir.dt.float32
BF16 = mybir.dt.bfloat16
I32 = mybir.dt.int32
U32 = mybir.dt.uint32
U8 = mybir.dt.uint8
FP8X4 = mybir.dt.float8_e4m3fn_x4
ALU = mybir.AluOpType
ACT = mybir.ActivationFunctionType

P = 128
B, S, D, H, HD = 2, 256, 1024, 8, 128
ROT = HD // 4
HALF = ROT // 2
EPS = 1e-5
ROPE_BASE = 10000.0
PACK = 4
PASSES = D // (P * PACK)
K_CHUNKS = D // P
PARITY = S // P
HEAD_COLS = 3 * HD
QK_COLS = 2 * HD
PAIRS = 3
SINGLES = (6, 7)
UNIT_COLS = 2 * HEAD_COLS
UNITS = 2 * PAIRS + len(SINGLES)
WIDE_BLOCKS = 4
WIDE_COLS = WIDE_BLOCKS * HD
BLOCKS = 3 * H
BN_FMAX = 512
BN_STATS_DIM = 6
ROUND_MAGIC = 1.5 * 2.0**23

FLOPS = 2 * B * S * D * 3 * H * HD


def regroup(copy, dst, src):
    copy(
        out=dst.rearrange("p (c i) t -> p c t i", i=4),
        in_=src.rearrange("p t (c i) -> p c t i", i=4),
    )


def tile_customgptneoxlayer_pa_kernel(
    tc, hidden_states, ln1_g, ln1_b, W_qkv, b_qkv, out_0, out_1, out_2
):
    nc = tc.nc
    outs = (out_0, out_1, out_2)
    with ExitStack() as stack:
        consts = stack.enter_context(tc.tile_pool(name="consts", bufs=1))
        xpool = stack.enter_context(tc.tile_pool(name="xpool", bufs=1))
        wpool = stack.enter_context(tc.tile_pool(name="wpool", bufs=1))
        stage = stack.enter_context(tc.tile_pool(name="stage", bufs=4))
        respool = stack.enter_context(tc.tile_pool(name="respool", bufs=1))
        ropepool = stack.enter_context(tc.tile_pool(name="ropepool", bufs=2))
        psum = stack.enter_context(tc.psum_pool(name="psum", bufs=8))
        stack.enter_context(tc.manual_schedule())

        gain_raw = consts.tile([P, PASSES, PACK], BF16)
        shift_raw = consts.tile([P, PASSES, PACK], BF16)
        bias_bc = consts.tile([P, BLOCKS, HD], BF16)
        x_sb = [xpool.tile([P, PARITY, D], BF16, name="x_sb%d" % b) for b in range(B)]
        xn = [xpool.tile([P, PARITY, D], F32, name="xn%d" % b) for b in range(B)]
        xb = xpool.tile([P, B, K_CHUNKS, S], BF16)
        xcodes = xpool.tile([P, B, PASSES, S], U32, align_bytes=64)
        xscales = xpool.tile([P, B, PASSES, S], U8, align_bytes=64)
        w_codes = [wpool.tile([P, UNIT_COLS], U32, name="w_codes%d" % u, align_bytes=64) for u in range(UNITS)]
        w_scales = [wpool.tile([P, UNIT_COLS], U8, name="w_scales%d" % u, align_bytes=64) for u in range(UNITS)]
        res = [
            respool.tile([P, B, 2 if i < PAIRS else 1, 3, PARITY, HD], F32, name="res%d" % i)
            for i in range(PAIRS + len(SINGLES))
        ]

        def load_x(b, *parities):
            rows = hidden_states[b].rearrange("(p e) d -> p e d", e=PARITY)
            for e in parities or range(PARITY):
                nc.sync.dma_start(out=x_sb[b][:, e, :], in_=rows[:, e, :])

        w_rows = W_qkv.rearrange("(g p t) n -> g p t n", t=PACK, p=P)
        wraw = {}

        def load_w(pair, g):
            tile = wpool.tile([P, PACK, UNIT_COLS], BF16, name="wraw%d_%d" % (pair, g))
            cols = slice(UNIT_COLS * pair, UNIT_COLS * (pair + 1))
            nc.sync.dma_start(out=tile[:], in_=w_rows[g][:, :, cols])
            wraw[pair, g] = tile

        load_x(0)
        load_w(0, 0)
        load_x(1)
        for raw, param in ((gain_raw, ln1_g), (shift_raw, ln1_b)):
            nc.sync.dma_start(out=raw[:], in_=param.rearrange("(g p t) -> p g t", t=PACK, p=P))
        load_w(0, 1)
        for pair in range(1, H // 2):
            for g in range(PASSES):
                load_w(pair, g)
                if (pair, g) == (1, 0):
                    nc.sync.dma_start(
                        out=bias_bc[:].rearrange("p n d -> p (n d)"), in_=b_qkv.partition_broadcast(P)
                    )

        pos_i = consts.tile([P, PARITY], I32)
        nc.gpsimd.iota(pos_i[:], pattern=[[1, PARITY]], base=0, channel_multiplier=PARITY)
        ident_f32 = consts.tile([P, P], F32)
        make_identity(nc, ident_f32[:])
        neg_half = consts.tile([P, PARITY], F32)
        nc.vector.memset(neg_half[:], -0.5)

        pos = consts.tile([P, PARITY], F32)
        nc.vector.tensor_copy(out=pos[:], in_=pos_i[:])
        turns = consts.tile([P, 2, PARITY, HALF], F32)
        for j in range(HALF):
            nc.vector.tensor_scalar(
                out=turns[:, 1, :, j],
                in0=pos[:],
                scalar1=ROPE_BASE ** (-j / HALF) / (2.0 * math.pi),
                scalar2=None,
                op0=ALU.mult,
            )
        nc.vector.tensor_scalar(
            out=turns[:, 0], in0=turns[:, 1], scalar1=0.25, scalar2=None, op0=ALU.add
        )
        whole = consts.tile([P, 2, PARITY, HALF], F32)
        nc.vector.tensor_scalar(
            out=whole[:],
            in0=turns[:],
            scalar1=ROUND_MAGIC,
            scalar2=ROUND_MAGIC,
            op0=ALU.add,
            op1=ALU.subtract,
        )
        frac = consts.tile([P, 2, PARITY, HALF], F32)
        nc.vector.tensor_tensor(out=frac[:], in0=turns[:], in1=whole[:], op=ALU.subtract)
        cos_tab = consts.tile([P, PARITY, 2, HALF], F32)
        sin_tab = consts.tile([P, PARITY, 2, HALF], F32)
        nc.scalar.activation(
            out=cos_tab[:],
            in_=frac[:, 0].unsqueeze(2).to_broadcast([P, PARITY, 2, HALF]),
            func=ACT.Sin,
            scale=2.0 * math.pi,
        )
        nc.scalar.activation(
            out=sin_tab[:, :, 0, :], in_=frac[:, 1], func=ACT.Sin, scale=-2.0 * math.pi
        )
        nc.scalar.activation(
            out=sin_tab[:, :, 1, :], in_=frac[:, 1], func=ACT.Sin, scale=2.0 * math.pi
        )
        cos_qk = consts.tile([P, 2, PARITY, ROT], F32)
        sin_qk = consts.tile([P, 2, PARITY, ROT], F32)
        gb_cols = consts.tile([P, 2 * K_CHUNKS], F32)

        def normalise(b, fillers):
            stats = xpool.tile([P, PARITY, D // BN_FMAX, BN_STATS_DIM], F32, name="stats%d" % b)
            mean_var = xpool.tile([P, PARITY, 2], F32, name="mean_var%d" % b)

            def partial(e, f):
                nc.vector.bn_stats(
                    out=stats[:, e, f, :], in_=x_sb[b][:, e, BN_FMAX * f : BN_FMAX * (f + 1)]
                )

            def aggregate(e):
                nc.vector.bn_aggr(
                    out=mean_var[:, e, :], in_=stats[:, e].rearrange("p f s -> p (f s)")
                )

            partial(0, 0)
            partial(0, 1)
            partial(1, 0)
            aggregate(0)
            partial(1, 1)
            fillers[0]()
            aggregate(1)
            fillers[1]()
            neg_mean = xpool.tile([P, PARITY], F32, name="neg_mean%d" % b)
            nc.vector.tensor_scalar(
                out=neg_mean[:], in0=mean_var[:, :, 0], scalar1=-1.0, scalar2=None, op0=ALU.mult
            )
            var_eps = xpool.tile([P, PARITY], F32, name="var_eps%d" % b)
            nc.vector.tensor_scalar(
                out=var_eps[:], in0=mean_var[:, :, 1], scalar1=EPS, scalar2=None, op0=ALU.add
            )
            rstd = xpool.tile([P, PARITY], F32, name="rstd%d" % b)
            nc.gpsimd.tensor_tensor(out=rstd[:], in0=var_eps[:], in1=neg_half[:], op=ALU.pow)
            for e in range(PARITY):
                nc.gpsimd.tensor_scalar(
                    out=xn[b][:, e, :].rearrange("p (g t q) -> p g t q", g=PASSES, t=PACK),
                    in0=x_sb[b][:, e, :].rearrange("p (g q t) -> p g t q", g=PASSES, t=PACK),
                    scalar1=neg_mean[:, e : e + 1],
                    scalar2=rstd[:, e : e + 1],
                    op0=ALU.add,
                    op1=ALU.mult,
                )

        def transpose_x(b):
            for i in range(K_CHUNKS // 2):
                xt = psum.tile([P, 2, S], F32, tag="bank", name="xt%d_%d" % (b, i))
                for ai in range(2):
                    a = 2 * i + ai
                    for e in range(PARITY):
                        nc.tensor.transpose(
                            xt[:, ai, P * e : P * (e + 1)],
                            xn[b][:, e, P * a : P * (a + 1)],
                            ident_f32[:],
                        )
                for ai in range(2):
                    a = 2 * i + ai
                    gain = gb_cols[:, a : a + 1]
                    shift = gb_cols[:, K_CHUNKS + a : K_CHUNKS + a + 1]
                    nc.vector.tensor_scalar(
                        out=xb[:, b, a, :],
                        in0=xt[:, ai, :],
                        scalar1=gain,
                        scalar2=shift,
                        op0=ALU.mult,
                        op1=ALU.add,
                    )

        xgroups = {}

        def regroup_x(b):
            xgroups[b] = xpool.tile([P, PASSES, S, PACK], BF16, name="xg%d" % b, align_bytes=64)
            nc.vector.tensor_copy(
                out=xgroups[b][:].rearrange("p g (c i) t -> p g c t i", i=4),
                in_=xb[:, b].rearrange("p (g t) (c i) -> p g c t i", t=PACK, i=4),
            )

        def quantise_x(b):
            nc.vector.quantize_mx(
                out=xcodes[:, b].rearrange("p g c -> p (g c)").bitcast(FP8X4),
                scales=xscales[:, b].rearrange("p g c -> p (g c)"),
                in_=xgroups[b][:].rearrange("p g c t -> p (g c t)"),
            )

        wgroups = {}

        def regroup_w(u):
            wgroups[u] = stage.tile([P, UNIT_COLS, PACK], BF16, align_bytes=64, name="wg")
            if u < 2 * PAIRS:
                regroup(nc.scalar.copy, wgroups[u][:], wraw[u // 2, u % 2][:])
            else:
                h = SINGLES[u - 2 * PAIRS]
                cols = slice(HEAD_COLS * (h % 2), HEAD_COLS * (h % 2 + 1))
                for g in range(PASSES):
                    regroup(nc.scalar.copy, wgroups[u][:, HEAD_COLS * g : HEAD_COLS * (g + 1), :], wraw[h // 2, g][:, :, cols])

        def quantise_w(u, pieces=(slice(0, 512), slice(512, 768))):
            for cols in pieces:
                nc.vector.quantize_mx(
                    out=w_codes[u][:, cols].bitcast(FP8X4),
                    scales=w_scales[u][:, cols],
                    in_=wgroups[u][:, cols, :].rearrange("p c t -> p (c t)"),
                )

        def mx_group(acc, b, e, operands):
            tokens = slice(P * e, P * (e + 1))
            for g, (u, cols) in enumerate(operands):
                nc.tensor.matmul_mx(
                    out=acc,
                    lhsT=xcodes[:, b, g, tokens].bitcast(FP8X4),
                    lhsT_scale=xscales[:, b, g, tokens],
                    rhs=w_codes[u][:, cols].bitcast(FP8X4),
                    rhs_scale=w_scales[u][:, cols],
                    start=(g == 0),
                    stop=(g == PASSES - 1),
                )

        def store(i, w, batches=slice(0, B)):
            if i < PAIRS:
                for b in range(batches.start, batches.stop):
                    nc.sync.dma_start(
                        out=outs[w][b, 2 * i : 2 * i + 2].rearrange("h (p e) d -> p h (e d)", e=PARITY),
                        in_=res[i][:, b, :, w].rearrange("p h e d -> p h (e d)"),
                    )
            else:
                nc.sync.dma_start(
                    out=outs[w][batches, SINGLES[i - PAIRS]].rearrange("b (p e) d -> p b (e d)", e=PARITY),
                    in_=res[i][:, batches, 0, w].rearrange("p b e d -> p b (e d)"),
                )

        def store_qk(i, batches=slice(0, B)):
            store(i, 0, batches)
            store(i, 1, batches)

        accs = {}

        def multiply_pair(i, b):
            acc_wide = []
            for e in range(PARITY):
                acc = psum.tile([P, WIDE_BLOCKS, HD], F32, tag="bank", name="acc_wide%d" % e)
                operands = [(2 * i + g, slice(0, WIDE_COLS)) for g in range(PASSES)]
                mx_group(acc[:].rearrange("p n d -> p (n d)"), b, e, operands)
                acc_wide.append(acc)
            acc_narrow = psum.tile([P, PARITY, 2, HD], F32, tag="bank", name="acc_narrow")
            for e in range(PARITY):
                operands = [(2 * i + g, slice(WIDE_COLS, UNIT_COLS)) for g in range(PASSES)]
                mx_group(acc_narrow[:, e].rearrange("p n d -> p (n d)"), b, e, operands)
            accs[i, b] = acc_wide, acc_narrow

        def leave_pair(i, b):
            leave_wide(i, b)
            leave_narrow(i, b)

        def leave_wide(i, b):
            acc_wide, acc_narrow = accs[i, b]
            first = 6 * i
            blocks = res[i][:, b].rearrange("p h w e d -> p (h w) e d")
            for e in range(PARITY):
                nc.vector.tensor_tensor(
                    out=blocks[:, 0:WIDE_BLOCKS, e, :],
                    in0=acc_wide[e][:],
                    in1=bias_bc[:, first : first + WIDE_BLOCKS, :],
                    op=ALU.add,
                )

        def leave_narrow(i, b):
            acc_wide, acc_narrow = accs[i, b]
            first = 6 * i
            blocks = res[i][:, b].rearrange("p h w e d -> p (h w) e d")
            nc.vector.tensor_tensor(
                out=blocks[:, WIDE_BLOCKS:6].rearrange("p n e d -> p e n d"),
                in0=acc_narrow[:],
                in1=bias_bc[:, first + WIDE_BLOCKS : first + 6, :]
                .unsqueeze(1)
                .to_broadcast([P, PARITY, 2, HD]),
                op=ALU.add,
            )
            store(i, 2, slice(b, b + 1))

        def multiply_single(i):
            u = PAIRS + i
            for b in range(B):
                bank = psum.tile([P, PARITY, 2, HD], F32, tag="bank", name="acc_qk")
                operands = [(u, slice(HEAD_COLS * g, HEAD_COLS * g + QK_COLS)) for g in range(PASSES)]
                for e in range(PARITY):
                    mx_group(bank[:, e].rearrange("p n d -> p (n d)"), b, e, operands)
                accs[i, b] = bank
            bank = psum.tile([P, B, PARITY, HD], F32, tag="bank", name="acc_val")
            operands = [(u, slice(HEAD_COLS * g + QK_COLS, HEAD_COLS * (g + 1))) for g in range(PASSES)]
            for b in range(B):
                for e in range(PARITY):
                    mx_group(bank[:, b, e], b, e, operands)
            accs[i, "val"] = bank

        def leave_qk(i, b):
            first = 3 * SINGLES[i - PAIRS]
            nc.vector.tensor_tensor(
                out=res[i][:, b, 0, 0:2].rearrange("p w e d -> p e w d"),
                in0=accs[i, b][:],
                in1=bias_bc[:, first : first + 2, :].unsqueeze(1).to_broadcast([P, PARITY, 2, HD]),
                op=ALU.add,
            )

        def leave_val(i):
            first = 3 * SINGLES[i - PAIRS] + 2
            nc.vector.tensor_tensor(
                out=res[i][:, :, 0, 2],
                in0=accs[i, "val"][:],
                in1=bias_bc[:, first : first + 1, :].unsqueeze(1).to_broadcast([P, B, PARITY, HD]),
                op=ALU.add,
            )
            store(i, 2)

        def rotation(engine, i, b):
            u = res[i][:, b : b + 1, :, 0:2, :, 0:ROT].rearrange("p b h w e j -> p (b h) (w e) j")
            shape = list(u.shape)
            cos_b = cos_qk[:].rearrange("p w e j -> p (w e) j").unsqueeze(1).to_broadcast(shape)
            sin_b = sin_qk[:].rearrange("p w e j -> p (w e) j").unsqueeze(1).to_broadcast(shape)
            who = "v" if engine is nc.vector else "g"
            straight = ropepool.tile(shape, F32, name="straight_%s%d" % (who, shape[1]))
            crossed = ropepool.tile(shape, F32, name="crossed_%s%d" % (who, shape[1]))

            def first():
                engine.tensor_tensor(out=straight[:], in0=u, in1=cos_b, op=ALU.mult)

            def second():
                if shape[1] == 1:
                    swapped = u.rearrange("p a c (z j) -> p a c z j", z=2)[:, :, :, ::-1, :]
                    engine.tensor_tensor(
                        out=crossed[:].rearrange("p a c (z j) -> p a c z j", z=2),
                        in0=swapped,
                        in1=sin_b.rearrange("p a c (z j) -> p a c z j", z=2),
                        op=ALU.mult,
                    )
                    return
                for to, of in ((slice(0, HALF), slice(HALF, ROT)), (slice(HALF, ROT), slice(0, HALF))):
                    engine.tensor_tensor(
                        out=crossed[:, :, :, to],
                        in0=u[:, :, :, of],
                        in1=sin_b[:, :, :, to],
                        op=ALU.mult,
                    )

            def third():
                engine.tensor_tensor(out=u, in0=straight[:], in1=crossed[:], op=ALU.add)

            return first, second, third

        def columns(i, raw):
            nc.vector.tensor_copy(
                out=gb_cols[:, K_CHUNKS * i : K_CHUNKS * (i + 1)],
                in_=raw[:].rearrange("p g t -> p (g t)"),
            )

        def double(twice, tab):
            nc.vector.tensor_copy(
                out=twice[:],
                in_=tab[:]
                .rearrange("p e s j -> p e (s j)")
                .unsqueeze(1)
                .to_broadcast([P, 2, PARITY, ROT]),
            )

        wide, narrow = slice(0, 512), slice(512, 768)

        def rotate_gpsimd(n):
            for step in rotation(nc.gpsimd, n // B, n % B):
                step()

        def late_store(n):
            if 0 <= n < 5:
                store_qk(n // B, slice(n % B, n % B + 1))

        normalise(0, (lambda: double(cos_qk, cos_tab), lambda: double(sin_qk, sin_tab)))
        normalise(1, (lambda: columns(0, gain_raw), lambda: columns(1, shift_raw)))
        regroup_w(0)
        quantise_w(0)
        transpose_x(0)
        regroup_w(1)
        quantise_w(1, (narrow,))
        regroup_x(0)
        quantise_w(1, (wide,))
        quantise_x(0)
        transpose_x(1)
        multiply_pair(0, 0)
        leave_wide(0, 0)
        regroup_x(1)
        leave_narrow(0, 0)
        rotate_gpsimd(0)
        regroup_w(2)
        quantise_x(1)
        quantise_w(2)
        multiply_pair(0, 1)
        regroup_w(3)
        quantise_w(3)
        leave_pair(0, 1)
        rotate_gpsimd(1)

        for n in range(2, B * PAIRS - 1):
            i, b = divmod(n, B)
            regroup_w(n + 2)
            quantise_w(n + 2)
            multiply_pair(i, b)
            leave_pair(i, b)
            rotate_gpsimd(n)
            late_store(n - 2)
        regroup_w(7)
        multiply_pair(2, 1)
        multiply_single(PAIRS)
        leave_pair(2, 1)
        quantise_w(7, (wide,))
        first, second, third = rotation(nc.vector, 2, 1)
        first()
        second()
        quantise_w(7, (narrow,))
        third()
        store_qk(2, slice(1, 2))
        multiply_single(PAIRS + 1)
        late_store(3)
        for i in (PAIRS, PAIRS + 1):
            leave_qk(i, 0)
            leave_qk(i, 1)
            steps = [rotation(nc.vector, i, b) for b in range(B)]
            for step in range(2):
                for b in range(B):
                    steps[b][step]()
            leave_val(i)
            for b in range(B):
                steps[b][2]()
                store_qk(i, slice(b, b + 1))
            if i == PAIRS:
                late_store(4)
